import numpy as np
import ml_dtypes


def mxq(x, axis, fmt="e4m3"):
    dtype, down = {"e4m3": (ml_dtypes.float8_e4m3fn, 7), "e5m2": (ml_dtypes.float8_e5m2, 14)}[fmt]
    v = np.moveaxis(np.asarray(x, np.float32).astype(ml_dtypes.bfloat16).astype(np.float64), axis, -1)
    blocks = v.reshape(v.shape[:-1] + (-1, 32))
    amax = np.abs(blocks).max(-1, keepdims=True)
    byte = np.maximum(np.where(amax > 0, np.frexp(amax)[1] - 1 + 127, 0) - down, 1)
    scale = np.exp2(byte - 127.0)
    codes = (blocks / scale).astype(np.float32).astype(dtype).astype(np.float64)
    return np.moveaxis((codes * scale).reshape(v.shape), -1, axis)


BF16 = ml_dtypes.bfloat16


def bf(x):
    return np.asarray(x, np.float32).astype(BF16)


def f64(x):
    return np.asarray(x).astype(np.float64)


T, I, O = 4096, 512, 1024


def bit_sign(v):
    return np.where(v > 0, 1.0, -1.0)


def setup_inputs():
    x = np.random.standard_normal((T, I))
    weight = np.random.standard_normal((O, I)) * 0.01
    g = np.random.standard_normal((T, O)) * np.exp2(np.random.randint(-12, 1, (T, 1))) * 4.0
    return {"x": bf(x), "weight": bf(weight), "grad_out": bf(g)}


def reference(x, weight, grad_out):
    w_bin = bit_sign(f64(weight))
    div = I ** 0.5
    return (mxq(f64(grad_out), 1, "e5m2") @ mxq(w_bin, 0, "e4m3")) / div

@@ -1,0 +1,162 @@
+import math
+from contextlib import ExitStack
+
+import concourse.mybir as mybir
+from concourse.masks import make_identity
+
+T, I, O = 4096, 512, 1024
+FLOPS = 2 * T * I * O
+BYTES = T * O * 2 + O * I * 2 + T * I * 4
+
+P = 128
+BF16 = mybir.dt.bfloat16
+F32 = mybir.dt.float32
+U32 = mybir.dt.uint32
+U8 = mybir.dt.uint8
+E4 = mybir.dt.float8_e4m3fn_x4
+E5 = mybir.dt.float8_e5m2_x4
+ALU = mybir.AluOpType
+ACT = mybir.ActivationFunctionType
+
+SIZES = [1, 1, 2, 4, 4, 4, 4, 4, 4, 2, 1, 1]
+LEAD = [2, 2, 3, 4, 5, 6, 7, 8, 11, 11, 11, 11]
+HEAD = 3
+TAIL = 8
+INV = 1.0 / math.sqrt(I)
+
+
+def tile_blinear_t_kernel(tc, x, weight, grad_out, out):
+    nc = tc.nc
+    nchunks = len(SIZES)
+    starts = [P * sum(SIZES[:c]) for c in range(nchunks)]
+    with ExitStack() as ctx:
+        const = ctx.enter_context(tc.tile_pool(name="const", bufs=1))
+        gpool = ctx.enter_context(tc.tile_pool(name="gpool", bufs=1))
+        opool = ctx.enter_context(tc.tile_pool(name="opool", bufs=1))
+        spool = ctx.enter_context(tc.tile_pool(name="spool", bufs=4))
+        xpool = ctx.enter_context(tc.psum_pool(name="xpool", bufs=4))
+        apool = ctx.enter_context(tc.psum_pool(name="apool", bufs=4))
+        ctx.enter_context(tc.manual_schedule())
+
+        w_view = weight.rearrange("(q p e) c -> q p (e c)", q=4, p=P, e=2)
+        w_raw = []
+        for q in range(4):
+            wr = const.tile([P, 2 * I], BF16, name="w_raw%d" % q)
+            nc.sync.dma_start(out=wr[:], in_=w_view[q])
+            w_raw.append(wr)
+        g_sb = []
+        for c in range(nchunks):
+            n = SIZES[c]
+            gt = gpool.tile([P, n * O], BF16, name="g%d" % c)
+            nc.sync.dma_start(
+                out=gt[:],
+                in_=grad_out[starts[c] : starts[c] + P * n, :].rearrange("(p j) o -> p (j o)", j=n),
+            )
+            g_sb.append(gt)
+
+        ident = const.tile([P, P], F32, name="ident")
+        make_identity(nc, ident[:])
+        warm = const.tile([P, 2], F32, name="warm")
+        nc.vector.memset(warm[:, 0:1], 0.0)
+        nc.scalar.activation(out=warm[:, 1:2], in_=warm[:, 0:1], func=ACT.Copy, scale=1.0)
+
+        w_grp = []
+        for g in range(2):
+            two = const.tile([P, 4, I], BF16, name="w_two%d" % g)
+            for u in range(2):
+                nc.vector.tensor_scalar(
+                    out=two[:, 2 * u : 2 * u + 2, :],
+                    in0=w_raw[2 * g + u][:].rearrange("p (e c) -> p e c", e=2),
+                    scalar1=0.0,
+                    scalar2=2.0,
+                    op0=ALU.is_gt,
+                    op1=ALU.mult,
+                )
+            grp = const.tile([P, I, 4], BF16, name="w_grp%d" % g, align_bytes=64)
+            nc.vector.tensor_scalar(
+                out=grp[:].rearrange("p (c i) t -> p c t i", i=4),
+                in0=two[:].rearrange("p t (c i) -> p c t i", i=4),
+                scalar1=-1.0,
+                scalar2=None,
+                op0=ALU.add,
+            )
+            w_grp.append(grp)
+        w_codes = []
+        w_scl = []
+        for g in range(2):
+            wc = const.tile([P, I], U32, name="w_codes%d" % g, align_bytes=64)
+            ws = const.tile([P, I], U8, name="w_scl%d" % g, align_bytes=64)
+            nc.vector.quantize_mx(
+                out=wc[:].bitcast(E4), scales=ws[:], in_=w_grp[g][:].rearrange("p c t -> p (c t)")
+            )
+            w_codes.append(wc)
+            w_scl.append(ws)
+
+        codes = {}
+        scl = {}
+
+        def flip(c):
+            n = SIZES[c]
+            words = g_sb[c][:].bitcast(F32)
+            grp = spool.tile([P, n * O], BF16, name="grp%d" % c, tag="grp", align_bytes=64)
+            gv = grp[:].bitcast(F32).rearrange("p (j g r u) -> p j g r u", j=n, g=2, r=P, u=2)
+            banks = []
+            for j in range(n):
+                xt = xpool.tile([P, 4, P], F32, name="xt%d_%d" % (c, j), tag="xt")
+                for q in range(4):
+                    lo = j * (O // 2) + q * P
+                    nc.tensor.transpose(xt[:, q, :], words[:, lo : lo + P], ident[:])
+                banks.append(xt)
+            for j in range(n):
+                src = banks[j][:].rearrange("p (g u) r -> p g r u", u=2)
+                on_scalar = c < HEAD or j == n - 1
+                if on_scalar:
+                    nc.scalar.copy(out=gv[:, j], in_=src)
+                else:
+                    nc.vector.tensor_copy(out=gv[:, j], in_=src)
+            cd = spool.tile([P, n * 256], U32, name="codes%d" % c, tag="codes", align_bytes=64)
+            sc = spool.tile([P, n * 256], U8, name="scl%d" % c, tag="scl", align_bytes=64)
+            pieces = 2 if n == 4 else 1
+            w = n // pieces
+            for h in range(pieces):
+                nc.vector.quantize_mx(
+                    out=cd[:, h * w * 256 : (h + 1) * w * 256].bitcast(E5),
+                    scales=sc[:, h * w * 256 : (h + 1) * w * 256],
+                    in_=grp[:, h * w * O : (h + 1) * w * O],
+                )
+            codes[c] = cd
+            scl[c] = sc
+
+        def multiply(c):
+            n = SIZES[c]
+            res = opool.tile([P, n, I], F32, name="res%d" % c)
+            for j in range(n):
+                acc = apool.tile([P, I], F32, name="acc%d_%d" % (c, j), tag="acc")
+                for g in range(2):
+                    lo = j * 256 + g * P
+                    nc.tensor.matmul_mx(
+                        out=acc[:],
+                        lhsT=codes[c][:, lo : lo + P].bitcast(E5),
+                        lhsT_scale=scl[c][:, lo : lo + P],
+                        rhs=w_codes[g][:].bitcast(E4),
+                        rhs_scale=w_scl[g][:],
+                        start=(g == 0),
+                        stop=(g == 1),
+                    )
+                if c >= TAIL and j % 2 == 1:
+                    nc.vector.tensor_scalar(
+                        out=res[:, j, :], in0=acc[:], scalar1=INV, scalar2=None, op0=ALU.mult
+                    )
+                else:
+                    nc.scalar.activation(out=res[:, j, :], in_=acc[:], func=ACT.Copy, scale=INV)
+            nc.sync.dma_start(
+                out=out[starts[c] : starts[c] + P * n, :].rearrange("(p j) i -> p j i", j=n),
+                in_=res[:],
+            )
+
+        flipped = 0
+        for c in range(nchunks):
+            while flipped <= LEAD[c]:
+                flip(flipped)
+                flipped += 1
+            multiply(c)

@@ -18,17 +18,31 @@ E5 = mybir.dt.float8_e5m2_x4
 ALU = mybir.AluOpType
 ACT = mybir.ActivationFunctionType
 
-SIZES = [1, 1, 2, 4, 4, 4, 4, 4, 4, 2, 1, 1]
-LEAD = [2, 2, 3, 4, 5, 6, 7, 8, 11, 11, 11, 11]
-HEAD = 3
-TAIL = 8
+NTILES = T // P
+ROWS = 8
+BUNCH = 4
+LOAD_PIECES = [1, 1, 2, 2, 2, 4, 4, 8, 8]
+STORE_PIECES = [8, 8, 4, 4, 2, 2, 2, 1, 1]
+V_COLS = 336
 INV = 1.0 / math.sqrt(I)
+
+
+def pieces_of(sizes):
+    table = {}
+    first = 0
+    for n in sizes:
+        for i in range(first, first + n):
+            table[i] = (first, n)
+        first += n
+    return table
 
 
 def tile_blinear_t_kernel(tc, x, weight, grad_out, out):
     nc = tc.nc
-    nchunks = len(SIZES)
-    starts = [P * sum(SIZES[:c]) for c in range(nchunks)]
+    load_of = pieces_of(LOAD_PIECES)
+    store_of = pieces_of(STORE_PIECES)
+    g_blocks = grad_out.rearrange("(k p j) o -> k p j o", p=P, j=ROWS)
+    o_blocks = out.rearrange("(k p j) i -> k p j i", p=P, j=ROWS)
     with ExitStack() as ctx:
         const = ctx.enter_context(tc.tile_pool(name="const", bufs=1))
         gpool = ctx.enter_context(tc.tile_pool(name="gpool", bufs=1))
@@ -38,21 +52,20 @@ def tile_blinear_t_kernel(tc, x, weight, grad_out, out):
         apool = ctx.enter_context(tc.psum_pool(name="apool", bufs=4))
         ctx.enter_context(tc.manual_schedule())
 
-        w_view = weight.rearrange("(q p e) c -> q p (e c)", q=4, p=P, e=2)
+        w_view = weight.rearrange("(q p e) c -> q p e c", q=4, p=P, e=2)
         w_raw = []
         for q in range(4):
-            wr = const.tile([P, 2 * I], BF16, name="w_raw%d" % q)
+            wr = const.tile([P, 2, I], BF16, name="w_raw%d" % q)
             nc.sync.dma_start(out=wr[:], in_=w_view[q])
             w_raw.append(wr)
-        g_sb = []
-        for c in range(nchunks):
-            n = SIZES[c]
-            gt = gpool.tile([P, n * O], BF16, name="g%d" % c)
-            nc.sync.dma_start(
-                out=gt[:],
-                in_=grad_out[starts[c] : starts[c] + P * n, :].rearrange("(p j) o -> p (j o)", j=n),
-            )
-            g_sb.append(gt)
+        g_sb = {}
+        first = 0
+        for n in LOAD_PIECES:
+            gt = gpool.tile([P, n, O], BF16, name="g%d" % first)
+            j0 = first % ROWS
+            nc.sync.dma_start(out=gt[:], in_=g_blocks[first // ROWS][:, j0 : j0 + n, :])
+            g_sb[first] = gt
+            first += n
 
         ident = const.tile([P, P], F32, name="ident")
         make_identity(nc, ident[:])
@@ -62,23 +75,29 @@ def tile_blinear_t_kernel(tc, x, weight, grad_out, out):
 
         w_grp = []
         for g in range(2):
-            two = const.tile([P, 4, I], BF16, name="w_two%d" % g)
+            half = const.tile([P, 4, I], BF16, name="w_half%d" % g)
             for u in range(2):
                 nc.vector.tensor_scalar(
-                    out=two[:, 2 * u : 2 * u + 2, :],
-                    in0=w_raw[2 * g + u][:].rearrange("p (e c) -> p e c", e=2),
+                    out=half[:, 2 * u : 2 * u + 2, :],
+                    in0=w_raw[2 * g + u][:],
                     scalar1=0.0,
-                    scalar2=2.0,
+                    scalar2=0.5,
                     op0=ALU.is_gt,
-                    op1=ALU.mult,
+                    op1=ALU.subtract,
                 )
             grp = const.tile([P, I, 4], BF16, name="w_grp%d" % g, align_bytes=64)
             nc.vector.tensor_scalar(
-                out=grp[:].rearrange("p (c i) t -> p c t i", i=4),
-                in0=two[:].rearrange("p t (c i) -> p c t i", i=4),
-                scalar1=-1.0,
+                out=grp[:, 0:V_COLS, :].rearrange("p (c i) t -> p c t i", i=4),
+                in0=half[:, :, 0:V_COLS].rearrange("p t (c i) -> p c t i", i=4),
+                scalar1=2.0,
                 scalar2=None,
-                op0=ALU.add,
+                op0=ALU.mult,
+            )
+            nc.scalar.activation(
+                out=grp[:, V_COLS:I, :].rearrange("p (c i) t -> p c t i", i=4),
+                in_=half[:, :, V_COLS:I].rearrange("p t (c i) -> p c t i", i=4),
+                func=ACT.Copy,
+                scale=2.0,
             )
             w_grp.append(grp)
         w_codes = []
@@ -94,69 +113,72 @@ def tile_blinear_t_kernel(tc, x, weight, grad_out, out):
 
         codes = {}
         scl = {}
+        res = {}
 
-        def flip(c):
-            n = SIZES[c]
-            words = g_sb[c][:].bitcast(F32)
-            grp = spool.tile([P, n * O], BF16, name="grp%d" % c, tag="grp", align_bytes=64)
-            gv = grp[:].bitcast(F32).rearrange("p (j g r u) -> p j g r u", j=n, g=2, r=P, u=2)
+        def flip(b):
+            grp = spool.tile([P, BUNCH * O], BF16, name="grp%d" % b, tag="grp", align_bytes=64)
+            gv = grp[:].bitcast(F32).rearrange("p (j g r u) -> p j g r u", j=BUNCH, g=2, r=P, u=2)
             banks = []
-            for j in range(n):
-                xt = xpool.tile([P, 4, P], F32, name="xt%d_%d" % (c, j), tag="xt")
+            for j in range(BUNCH):
+                i = b * BUNCH + j
+                lfirst = load_of[i][0]
+                words = g_sb[lfirst][:, i - lfirst, :].bitcast(F32)
+                xt = xpool.tile([P, 4, P], F32, name="xt%d" % i, tag="xt")
                 for q in range(4):
-                    lo = j * (O // 2) + q * P
-                    nc.tensor.transpose(xt[:, q, :], words[:, lo : lo + P], ident[:])
+                    nc.tensor.transpose(xt[:, q, :], words[:, q * P : (q + 1) * P], ident[:])
                 banks.append(xt)
-            for j in range(n):
+            for j in range(BUNCH):
                 src = banks[j][:].rearrange("p (g u) r -> p g r u", u=2)
-                on_scalar = c < HEAD or j == n - 1
-                if on_scalar:
+                if b == 0 or j == BUNCH - 1:
                     nc.scalar.copy(out=gv[:, j], in_=src)
                 else:
                     nc.vector.tensor_copy(out=gv[:, j], in_=src)
-            cd = spool.tile([P, n * 256], U32, name="codes%d" % c, tag="codes", align_bytes=64)
-            sc = spool.tile([P, n * 256], U8, name="scl%d" % c, tag="scl", align_bytes=64)
-            pieces = 2 if n == 4 else 1
-            w = n // pieces
-            for h in range(pieces):
+            cd = spool.tile([P, BUNCH * 256], U32, name="codes%d" % b, tag="codes", align_bytes=64)
+            sc = spool.tile([P, BUNCH * 256], U8, name="scl%d" % b, tag="scl", align_bytes=64)
+            w = 1 if b == 0 else 2
+            for h in range(BUNCH // w):
                 nc.vector.quantize_mx(
                     out=cd[:, h * w * 256 : (h + 1) * w * 256].bitcast(E5),
                     scales=sc[:, h * w * 256 : (h + 1) * w * 256],
                     in_=grp[:, h * w * O : (h + 1) * w * O],
                 )
-            codes[c] = cd
-            scl[c] = sc
+            codes[b] = cd
+            scl[b] = sc
 
-        def multiply(c):
-            n = SIZES[c]
-            res = opool.tile([P, n, I], F32, name="res%d" % c)
-            for j in range(n):
-                acc = apool.tile([P, I], F32, name="acc%d_%d" % (c, j), tag="acc")
+        def multiply(lo, hi):
+            for i in range(lo, hi):
+                b = i // BUNCH
+                sfirst, sn = store_of[i]
+                if i == sfirst:
+                    res[sfirst] = opool.tile([P, sn, I], F32, name="res%d" % sfirst)
+                acc = apool.tile([P, I], F32, name="acc%d" % i, tag="acc")
                 for g in range(2):
-                    lo = j * 256 + g * P
+                    c0 = (i % BUNCH) * 256 + g * P
                     nc.tensor.matmul_mx(
                         out=acc[:],
-                        lhsT=codes[c][:, lo : lo + P].bitcast(E5),
-                        lhsT_scale=scl[c][:, lo : lo + P],
+                        lhsT=codes[b][:, c0 : c0 + P].bitcast(E5),
+                        lhsT_scale=scl[b][:, c0 : c0 + P],
                         rhs=w_codes[g][:].bitcast(E4),
                         rhs_scale=w_scl[g][:],
                         start=(g == 0),
                         stop=(g == 1),
                     )
-                if c >= TAIL and j % 2 == 1:
-                    nc.vector.tensor_scalar(
-                        out=res[:, j, :], in0=acc[:], scalar1=INV, scalar2=None, op0=ALU.mult
-                    )
+                dst = res[sfirst][:, i - sfirst, :]
+                if i >= NTILES - BUNCH and i % 2 == 1:
+                    nc.vector.tensor_scalar(out=dst, in0=acc[:], scalar1=INV, scalar2=None, op0=ALU.mult)
                 else:
-                    nc.scalar.activation(out=res[:, j, :], in_=acc[:], func=ACT.Copy, scale=INV)
-            nc.sync.dma_start(
-                out=out[starts[c] : starts[c] + P * n, :].rearrange("(p j) i -> p j i", j=n),
-                in_=res[:],
-            )
+                    nc.scalar.activation(out=dst, in_=acc[:], func=ACT.Copy, scale=INV)
+                if i == sfirst + sn - 1:
+                    j0 = sfirst % ROWS
+                    nc.sync.dma_start(
+                        out=o_blocks[sfirst // ROWS][:, j0 : j0 + sn, :], in_=res[sfirst][:]
+                    )
 
-        flipped = 0
-        for c in range(nchunks):
-            while flipped <= LEAD[c]:
-                flip(flipped)
-                flipped += 1
-            multiply(c)
+        flip(0)
+        multiply(0, 2)
+        flip(1)
+        multiply(2, 4)
+        for b in range(2, NTILES // BUNCH):
+            flip(b)
+            multiply((b - 1) * BUNCH, b * BUNCH)
+        multiply(NTILES - BUNCH, NTILES)

@@ -25,6 +25,7 @@ LOAD_PIECES = [1, 1, 2, 2, 2, 4, 4, 8, 8]
 STORE_PIECES = [8, 8, 4, 4, 2, 2, 2, 1, 1]
 V_COLS = 336
 INV = 1.0 / math.sqrt(I)
+WARM_BEFORE = 10
 
 
 def pieces_of(sizes):
@@ -72,6 +73,16 @@ def tile_blinear_t_kernel(tc, x, weight, grad_out, out):
         warm = const.tile([P, 2], F32, name="warm")
         nc.vector.memset(warm[:, 0:1], 0.0)
         nc.scalar.activation(out=warm[:, 1:2], in_=warm[:, 0:1], func=ACT.Copy, scale=1.0)
+
+        zeros = const.tile([P, I], BF16, name="zeros")
+        nc.vector.memset(zeros[:], 0.0)
+        idle_ps = apool.tile([P, I], F32, name="idle_ps", tag="acc")
+
+        def dummy():
+            nc.tensor.matmul(out=idle_ps[:], lhsT=zeros[:, 0:P], rhs=zeros[:], start=True, stop=True)
+
+        for n in range(WARM_BEFORE):
+            dummy()
 
         w_grp = []
         for g in range(2):
@@ -126,6 +137,8 @@ def tile_blinear_t_kernel(tc, x, weight, grad_out, out):
                 xt = xpool.tile([P, 4, P], F32, name="xt%d" % i, tag="xt")
                 for q in range(4):
                     nc.tensor.transpose(xt[:, q, :], words[:, q * P : (q + 1) * P], ident[:])
+                if b == 0:
+                    dummy()
                 banks.append(xt)
             for j in range(BUNCH):
                 src = banks[j][:].rearrange("p (g u) r -> p g r u", u=2)

@@ -42,6 +42,7 @@ def tile_blinear_t_kernel(tc, x, weight, grad_out, out):
     nc = tc.nc
     load_of = pieces_of(LOAD_PIECES)
     store_of = pieces_of(STORE_PIECES)
+    store_firsts = sorted(set(first for first, count in store_of.values()))
     g_blocks = grad_out.rearrange("(k p j) o -> k p j o", p=P, j=ROWS)
     o_blocks = out.rearrange("(k p j) i -> k p j i", p=P, j=ROWS)
     with ExitStack() as ctx:
@@ -183,7 +184,8 @@ def tile_blinear_t_kernel(tc, x, weight, grad_out, out):
                     nc.scalar.activation(out=dst, in_=acc[:], func=ACT.Copy, scale=INV)
                 if i == sfirst + sn - 1:
                     j0 = sfirst % ROWS
-                    nc.sync.dma_start(
+                    queue = nc.scalar if store_firsts.index(sfirst) % 2 == 1 else nc.sync
+                    queue.dma_start(
                         out=o_blocks[sfirst // ROWS][:, j0 : j0 + sn, :], in_=res[sfirst][:]
                     )
 

@@ -57,13 +57,13 @@ def tile_blinear_t_kernel(tc, x, weight, grad_out, out):
         w_view = weight.rearrange("(q p e) c -> q p e c", q=4, p=P, e=2)
         w_raw = []
         for q in range(4):
-            wr = const.tile([P, 2, I], BF16, name="w_raw%d" % q)
+            wr = const.tile([P, 2, I], BF16, name="w_raw%d" % q, align_bytes=256)
             nc.sync.dma_start(out=wr[:], in_=w_view[q])
             w_raw.append(wr)
         g_sb = {}
         first = 0
         for n in LOAD_PIECES:
-            gt = gpool.tile([P, n, O], BF16, name="g%d" % first)
+            gt = gpool.tile([P, n, O], BF16, name="g%d" % first, align_bytes=256)
             j0 = first % ROWS
             nc.sync.dma_start(out=gt[:], in_=g_blocks[first // ROWS][:, j0 : j0 + n, :])
             g_sb[first] = gt
@@ -164,7 +164,7 @@ def tile_blinear_t_kernel(tc, x, weight, grad_out, out):
                 b = i // BUNCH
                 sfirst, sn = store_of[i]
                 if i == sfirst:
-                    res[sfirst] = opool.tile([P, sn, I], F32, name="res%d" % sfirst)
+                    res[sfirst] = opool.tile([P, sn, I], F32, name="res%d" % sfirst, align_bytes=256)
                 acc = apool.tile([P, I], F32, name="acc%d" % i, tag="acc")
                 for g in range(2):
                     c0 = (i % BUNCH) * 256 + g * P

@@ -69,13 +69,13 @@ def tile_blinear_t_kernel(tc, x, weight, grad_out, out):
             g_sb[first] = gt
             first += n
 
-        ident = const.tile([P, P], F32, name="ident")
+        ident = const.tile([P, P], F32, name="ident", align_bytes=256)
         make_identity(nc, ident[:])
         warm = const.tile([P, 2], F32, name="warm")
         nc.vector.memset(warm[:, 0:1], 0.0)
         nc.scalar.activation(out=warm[:, 1:2], in_=warm[:, 0:1], func=ACT.Copy, scale=1.0)
 
-        zeros = const.tile([P, I], BF16, name="zeros")
+        zeros = const.tile([P, I], BF16, name="zeros", align_bytes=256)
         nc.vector.memset(zeros[:], 0.0)
         idle_ps = apool.tile([P, I], F32, name="idle_ps", tag="acc")
 
@@ -87,7 +87,7 @@ def tile_blinear_t_kernel(tc, x, weight, grad_out, out):
 
         w_grp = []
         for g in range(2):
-            half = const.tile([P, 4, I], BF16, name="w_half%d" % g)
+            half = const.tile([P, 4, I], BF16, name="w_half%d" % g, align_bytes=256)
             for u in range(2):
                 nc.vector.tensor_scalar(
                     out=half[:, 2 * u : 2 * u + 2, :],
@@ -97,7 +97,7 @@ def tile_blinear_t_kernel(tc, x, weight, grad_out, out):
                     op0=ALU.is_gt,
                     op1=ALU.subtract,
                 )
-            grp = const.tile([P, I, 4], BF16, name="w_grp%d" % g, align_bytes=64)
+            grp = const.tile([P, I, 4], BF16, name="w_grp%d" % g, align_bytes=256)
             nc.vector.tensor_scalar(
                 out=grp[:, 0:V_COLS, :].rearrange("p (c i) t -> p c t i", i=4),
                 in0=half[:, :, 0:V_COLS].rearrange("p t (c i) -> p c t i", i=4),
@@ -115,8 +115,8 @@ def tile_blinear_t_kernel(tc, x, weight, grad_out, out):
         w_codes = []
         w_scl = []
         for g in range(2):
-            wc = const.tile([P, I], U32, name="w_codes%d" % g, align_bytes=64)
-            ws = const.tile([P, I], U8, name="w_scl%d" % g, align_bytes=64)
+            wc = const.tile([P, I], U32, name="w_codes%d" % g, align_bytes=256)
+            ws = const.tile([P, I], U8, name="w_scl%d" % g, align_bytes=256)
             nc.vector.quantize_mx(
                 out=wc[:].bitcast(E4), scales=ws[:], in_=w_grp[g][:].rearrange("p c t -> p (c t)")
             )
@@ -128,7 +128,7 @@ def tile_blinear_t_kernel(tc, x, weight, grad_out, out):
         res = {}
 
         def flip(b):
-            grp = spool.tile([P, BUNCH * O], BF16, name="grp%d" % b, tag="grp", align_bytes=64)
+            grp = spool.tile([P, BUNCH * O], BF16, name="grp%d" % b, tag="grp", align_bytes=256)
             gv = grp[:].bitcast(F32).rearrange("p (j g r u) -> p j g r u", j=BUNCH, g=2, r=P, u=2)
             banks = []
             for j in range(BUNCH):
@@ -147,8 +147,8 @@ def tile_blinear_t_kernel(tc, x, weight, grad_out, out):
                     nc.scalar.copy(out=gv[:, j], in_=src)
                 else:
                     nc.vector.tensor_copy(out=gv[:, j], in_=src)
-            cd = spool.tile([P, BUNCH * 256], U32, name="codes%d" % b, tag="codes", align_bytes=64)
-            sc = spool.tile([P, BUNCH * 256], U8, name="scl%d" % b, tag="scl", align_bytes=64)
+            cd = spool.tile([P, BUNCH * 256], U32, name="codes%d" % b, tag="codes", align_bytes=256)
+            sc = spool.tile([P, BUNCH * 256], U8, name="scl%d" % b, tag="scl", align_bytes=256)
             w = 1 if b == 0 else 2
             for h in range(BUNCH // w):
                 nc.vector.quantize_mx(

@@ -21,8 +21,8 @@ ACT = mybir.ActivationFunctionType
 NTILES = T // P
 ROWS = 8
 BUNCH = 4
-LOAD_PIECES = [1, 1, 2, 2, 2, 4, 4, 8, 8]
-STORE_PIECES = [8, 8, 4, 4, 2, 2, 2, 1, 1]
+LOAD_PIECES = [1, 1, 2, 4, 4, 4, 8, 8]
+STORE_PIECES = [8, 8, 4, 4, 2, 2, 2, 2]
 V_COLS = 336
 INV = 1.0 / math.sqrt(I)
 WARM_BEFORE = 10

@@ -21,9 +21,11 @@ ACT = mybir.ActivationFunctionType
 NTILES = T // P
 ROWS = 8
 BUNCH = 4
-LOAD_PIECES = [1, 1, 2, 4, 4, 4, 8, 8]
+LOAD_PIECES = [1, 1, 1, 1, 2, 2, 4, 4, 8, 8]
 STORE_PIECES = [8, 8, 4, 4, 2, 2, 2, 2]
-V_COLS = 336
+V_COLS = 256
+SIGN_SCALE = 2.0 ** 20
+SIGN_BIAS = -(2.0 ** -120)
 INV = 1.0 / math.sqrt(I)
 WARM_BEFORE = 10
 
@@ -73,7 +75,7 @@ def tile_blinear_t_kernel(tc, x, weight, grad_out, out):
         make_identity(nc, ident[:])
         warm = const.tile([P, 2], F32, name="warm")
         nc.vector.memset(warm[:, 0:1], 0.0)
-        nc.scalar.activation(out=warm[:, 1:2], in_=warm[:, 0:1], func=ACT.Copy, scale=1.0)
+        nc.scalar.activation(out=warm[:, 1:2], in_=warm[:, 0:1], func=ACT.Sign, scale=1.0)
 
         zeros = const.tile([P, I], BF16, name="zeros", align_bytes=256)
         nc.vector.memset(zeros[:], 0.0)
@@ -88,28 +90,29 @@ def tile_blinear_t_kernel(tc, x, weight, grad_out, out):
         w_grp = []
         for g in range(2):
             half = const.tile([P, 4, I], BF16, name="w_half%d" % g, align_bytes=256)
+            grp = const.tile([P, I, 4], BF16, name="w_grp%d" % g, align_bytes=256)
             for u in range(2):
                 nc.vector.tensor_scalar(
-                    out=half[:, 2 * u : 2 * u + 2, :],
-                    in0=w_raw[2 * g + u][:],
+                    out=half[:, 2 * u : 2 * u + 2, 0:V_COLS],
+                    in0=w_raw[2 * g + u][:, :, 0:V_COLS],
                     scalar1=0.0,
                     scalar2=0.5,
                     op0=ALU.is_gt,
                     op1=ALU.subtract,
                 )
-            grp = const.tile([P, I, 4], BF16, name="w_grp%d" % g, align_bytes=256)
+                nc.scalar.activation(
+                    out=grp[:, V_COLS:I, 2 * u : 2 * u + 2],
+                    in_=w_raw[2 * g + u][:, :, V_COLS:I].rearrange("p e c -> p c e"),
+                    func=ACT.Sign,
+                    scale=SIGN_SCALE,
+                    bias=SIGN_BIAS,
+                )
             nc.vector.tensor_scalar(
                 out=grp[:, 0:V_COLS, :].rearrange("p (c i) t -> p c t i", i=4),
                 in0=half[:, :, 0:V_COLS].rearrange("p t (c i) -> p c t i", i=4),
                 scalar1=2.0,
                 scalar2=None,
                 op0=ALU.mult,
-            )
-            nc.scalar.activation(
-                out=grp[:, V_COLS:I, :].rearrange("p (c i) t -> p c t i", i=4),
-                in_=half[:, :, V_COLS:I].rearrange("p t (c i) -> p c t i", i=4),
-                func=ACT.Copy,
-                scale=2.0,
             )
             w_grp.append(grp)
         w_codes = []

import math
from contextlib import ExitStack

import concourse.mybir as mybir
from concourse.masks import make_identity

T, I, O = 4096, 512, 1024
FLOPS = 2 * T * I * O
BYTES = T * O * 2 + O * I * 2 + T * I * 4

P = 128
BF16 = mybir.dt.bfloat16
F32 = mybir.dt.float32
U32 = mybir.dt.uint32
U8 = mybir.dt.uint8
E4 = mybir.dt.float8_e4m3fn_x4
E5 = mybir.dt.float8_e5m2_x4
ALU = mybir.AluOpType
ACT = mybir.ActivationFunctionType

NTILES = T // P
ROWS = 8
BUNCH = 4
LOAD_PIECES = [1, 1, 1, 1, 2, 2, 4, 4, 8, 8]
STORE_PIECES = [8, 8, 4, 4, 2, 2, 2, 2]
V_COLS = 256
SIGN_SCALE = 2.0 ** 20
SIGN_BIAS = -(2.0 ** -120)
INV = 1.0 / math.sqrt(I)
WARM_BEFORE = 10


def pieces_of(sizes):
    table = {}
    first = 0
    for n in sizes:
        for i in range(first, first + n):
            table[i] = (first, n)
        first += n
    return table


def tile_blinear_t_kernel(tc, x, weight, grad_out, out):
    nc = tc.nc
    load_of = pieces_of(LOAD_PIECES)
    store_of = pieces_of(STORE_PIECES)
    store_firsts = sorted(set(first for first, count in store_of.values()))
    g_blocks = grad_out.rearrange("(k p j) o -> k p j o", p=P, j=ROWS)
    o_blocks = out.rearrange("(k p j) i -> k p j i", p=P, j=ROWS)
    with ExitStack() as ctx:
        const = ctx.enter_context(tc.tile_pool(name="const", bufs=1))
        gpool = ctx.enter_context(tc.tile_pool(name="gpool", bufs=1))
        opool = ctx.enter_context(tc.tile_pool(name="opool", bufs=1))
        spool = ctx.enter_context(tc.tile_pool(name="spool", bufs=4))
        xpool = ctx.enter_context(tc.psum_pool(name="xpool", bufs=4))
        apool = ctx.enter_context(tc.psum_pool(name="apool", bufs=4))
        ctx.enter_context(tc.manual_schedule())

        w_view = weight.rearrange("(q p e) c -> q p e c", q=4, p=P, e=2)
        w_raw = []
        for q in range(4):
            wr = const.tile([P, 2, I], BF16, name="w_raw%d" % q, align_bytes=256)
            nc.sync.dma_start(out=wr[:], in_=w_view[q])
            w_raw.append(wr)
        g_sb = {}
        first = 0
        for n in LOAD_PIECES:
            gt = gpool.tile([P, n, O], BF16, name="g%d" % first, align_bytes=256)
            j0 = first % ROWS
            nc.sync.dma_start(out=gt[:], in_=g_blocks[first // ROWS][:, j0 : j0 + n, :])
            g_sb[first] = gt
            first += n

        ident = const.tile([P, P], F32, name="ident", align_bytes=256)
        make_identity(nc, ident[:])
        warm = const.tile([P, 2], F32, name="warm")
        nc.vector.memset(warm[:, 0:1], 0.0)
        nc.scalar.activation(out=warm[:, 1:2], in_=warm[:, 0:1], func=ACT.Sign, scale=1.0)

        zeros = const.tile([P, I], BF16, name="zeros", align_bytes=256)
        nc.vector.memset(zeros[:], 0.0)
        idle_ps = apool.tile([P, I], F32, name="idle_ps", tag="acc")

        def dummy():
            nc.tensor.matmul(out=idle_ps[:], lhsT=zeros[:, 0:P], rhs=zeros[:], start=True, stop=True)

        for n in range(WARM_BEFORE):
            dummy()

        w_grp = []
        for g in range(2):
            half = const.tile([P, 4, I], BF16, name="w_half%d" % g, align_bytes=256)
            grp = const.tile([P, I, 4], BF16, name="w_grp%d" % g, align_bytes=256)
            for u in range(2):
                nc.vector.tensor_scalar(
                    out=half[:, 2 * u : 2 * u + 2, 0:V_COLS],
                    in0=w_raw[2 * g + u][:, :, 0:V_COLS],
                    scalar1=0.0,
                    scalar2=0.5,
                    op0=ALU.is_gt,
                    op1=ALU.subtract,
                )
                nc.scalar.activation(
                    out=grp[:, V_COLS:I, 2 * u : 2 * u + 2],
                    in_=w_raw[2 * g + u][:, :, V_COLS:I].rearrange("p e c -> p c e"),
                    func=ACT.Sign,
                    scale=SIGN_SCALE,
                    bias=SIGN_BIAS,
                )
            nc.vector.tensor_scalar(
                out=grp[:, 0:V_COLS, :].rearrange("p (c i) t -> p c t i", i=4),
                in0=half[:, :, 0:V_COLS].rearrange("p t (c i) -> p c t i", i=4),
                scalar1=2.0,
                scalar2=None,
                op0=ALU.mult,
            )
            w_grp.append(grp)
        w_codes = []
        w_scl = []
        for g in range(2):
            wc = const.tile([P, I], U32, name="w_codes%d" % g, align_bytes=256)
            ws = const.tile([P, I], U8, name="w_scl%d" % g, align_bytes=256)
            nc.vector.quantize_mx(
                out=wc[:].bitcast(E4), scales=ws[:], in_=w_grp[g][:].rearrange("p c t -> p (c t)")
            )
            w_codes.append(wc)
            w_scl.append(ws)

        codes = {}
        scl = {}
        res = {}

        def flip(b):
            grp = spool.tile([P, BUNCH * O], BF16, name="grp%d" % b, tag="grp", align_bytes=256)
            gv = grp[:].bitcast(F32).rearrange("p (j g r u) -> p j g r u", j=BUNCH, g=2, r=P, u=2)
            banks = []
            for j in range(BUNCH):
                i = b * BUNCH + j
                lfirst = load_of[i][0]
                words = g_sb[lfirst][:, i - lfirst, :].bitcast(F32)
                xt = xpool.tile([P, 4, P], F32, name="xt%d" % i, tag="xt")
                for q in range(4):
                    nc.tensor.transpose(xt[:, q, :], words[:, q * P : (q + 1) * P], ident[:])
                if b == 0:
                    dummy()
                banks.append(xt)
            for j in range(BUNCH):
                src = banks[j][:].rearrange("p (g u) r -> p g r u", u=2)
                if b == 0 or j == BUNCH - 1:
                    nc.scalar.copy(out=gv[:, j], in_=src)
                else:
                    nc.vector.tensor_copy(out=gv[:, j], in_=src)
            cd = spool.tile([P, BUNCH * 256], U32, name="codes%d" % b, tag="codes", align_bytes=256)
            sc = spool.tile([P, BUNCH * 256], U8, name="scl%d" % b, tag="scl", align_bytes=256)
            w = 1 if b == 0 else 2
            for h in range(BUNCH // w):
                nc.vector.quantize_mx(
                    out=cd[:, h * w * 256 : (h + 1) * w * 256].bitcast(E5),
                    scales=sc[:, h * w * 256 : (h + 1) * w * 256],
                    in_=grp[:, h * w * O : (h + 1) * w * O],
                )
            codes[b] = cd
            scl[b] = sc

        def multiply(lo, hi):
            for i in range(lo, hi):
                b = i // BUNCH
                sfirst, sn = store_of[i]
                if i == sfirst:
                    res[sfirst] = opool.tile([P, sn, I], F32, name="res%d" % sfirst, align_bytes=256)
                acc = apool.tile([P, I], F32, name="acc%d" % i, tag="acc")
                for g in range(2):
                    c0 = (i % BUNCH) * 256 + g * P
                    nc.tensor.matmul_mx(
                        out=acc[:],
                        lhsT=codes[b][:, c0 : c0 + P].bitcast(E5),
                        lhsT_scale=scl[b][:, c0 : c0 + P],
                        rhs=w_codes[g][:].bitcast(E4),
                        rhs_scale=w_scl[g][:],
                        start=(g == 0),
                        stop=(g == 1),
                    )
                dst = res[sfirst][:, i - sfirst, :]
                if i >= NTILES - BUNCH and i % 2 == 1:
                    nc.vector.tensor_scalar(out=dst, in0=acc[:], scalar1=INV, scalar2=None, op0=ALU.mult)
                else:
                    nc.scalar.activation(out=dst, in_=acc[:], func=ACT.Copy, scale=INV)
                if i == sfirst + sn - 1:
                    j0 = sfirst % ROWS
                    queue = nc.scalar if store_firsts.index(sfirst) % 2 == 1 else nc.sync
                    queue.dma_start(
                        out=o_blocks[sfirst // ROWS][:, j0 : j0 + sn, :], in_=res[sfirst][:]
                    )

        flip(0)
        multiply(0, 2)
        flip(1)
        multiply(2, 4)
        for b in range(2, NTILES // BUNCH):
            flip(b)
            multiply((b - 1) * BUNCH, b * BUNCH)
        multiply(NTILES - BUNCH, NTILES)
